import numpy as np
import ml_dtypes


def mxq(x, axis, fmt="e4m3"):
    dtype, down = {"e4m3": (ml_dtypes.float8_e4m3fn, 7), "e5m2": (ml_dtypes.float8_e5m2, 14)}[fmt]
    v = np.moveaxis(np.asarray(x, np.float32).astype(ml_dtypes.bfloat16).astype(np.float64), axis, -1)
    blocks = v.reshape(v.shape[:-1] + (-1, 32))
    amax = np.abs(blocks).max(-1, keepdims=True)
    byte = np.maximum(np.where(amax > 0, np.frexp(amax)[1] - 1 + 127, 0) - down, 1)
    scale = np.exp2(byte - 127.0)
    codes = (blocks / scale).astype(np.float32).astype(dtype).astype(np.float64)
    return np.moveaxis((codes * scale).reshape(v.shape), -1, axis)


WIDE = False


def mx_kscale(k):
    if not WIDE:
        return np.ones(k)
    levels = np.array([10, -10, 5, -5, 0])
    a = np.random.permutation(np.resize(levels, k // 512 * 4)).reshape(k // 512, 4)
    idx = np.arange(k)
    return np.exp2(a[idx // 512, idx % 128 // 32])


BF16 = ml_dtypes.bfloat16


def bf(x):
    return np.asarray(x, np.float32).astype(BF16)


def f64(x):
    return np.asarray(x).astype(np.float64)


B, S, D_IN, D_OUT = 8, 2048, 512, 128


def relative_shift(x):
    b, s, d = x.shape
    padded = np.concatenate([np.zeros((b, 1, d)), x], axis=1).reshape(s + 1, b, d)
    return padded[1:].reshape(b, s, d)


def setup_inputs():
    s = mx_kscale(D_IN)
    return {"pos_embed": bf(np.random.standard_normal((B, S, D_IN)) * s),
            "W_r": bf(np.random.standard_normal((D_OUT, D_IN)) * 1.2 / np.sqrt(D_IN) / s[None, :]),
            "b_r": bf(np.random.standard_normal(D_OUT) * 0.3)}


def reference(pos_embed, W_r, b_r):
    shifted = relative_shift(f64(pos_embed))
    return (mxq(shifted, 2, "e4m3") @ mxq(f64(W_r), 1, "e4m3").T) + f64(b_r)

@@ -1,0 +1,166 @@
+from contextlib import ExitStack
+
+import concourse.mybir as mybir
+from concourse.masks import make_identity
+
+BF16 = mybir.dt.bfloat16
+F32 = mybir.dt.float32
+U32 = mybir.dt.uint32
+U8 = mybir.dt.uint8
+FP8X4 = mybir.dt.float8_e4m3fn_x4
+
+P = 128
+BATCHES = 8
+SEQ = 2048
+D_IN = 512
+D_OUT = 128
+PACK = 4
+BANK = 512
+
+HALVES = D_IN // 2 // P
+TILES = SEQ // P
+GROUP = 8
+GROUPS = TILES // GROUP
+FLIPPED_TILES = BANK // (HALVES * P)
+PRODUCT_TILES = BANK // D_OUT
+
+ZERO_ROWS = BATCHES - 1
+LEFT_ROWS = SEQ - ZERO_ROWS - (TILES - 1) * P
+assert LEFT_ROWS + ZERO_ROWS == P
+
+FLOPS = 2 * BATCHES * SEQ * D_IN * D_OUT
+
+
+def transpose_row_tile(nc, identity, flipped, row_tile):
+    words = row_tile.bitcast(F32)
+    for u in range(HALVES):
+        nc.tensor.transpose(flipped[:, u, :], words[:, u * P : (u + 1) * P], identity)
+
+
+def tile_relativemultiheadattention_pa_t_kernel(tc, pos_embed, W_r, b_r, out):
+    nc = tc.nc
+    pos_rows = pos_embed.flatten_outer_dims()
+    out_rows = out.flatten_outer_dims()
+
+    def whole_tiles(b):
+        return TILES - 1 if b == 0 else TILES
+
+    def first_row(b):
+        return ZERO_ROWS if b == 0 else SEQ * b
+
+    def batch_source(b):
+        rows = pos_rows[first_row(b) : first_row(b) + whole_tiles(b) * P, :]
+        return rows.rearrange("(p t) k -> p t k", t=whole_tiles(b))
+
+    def batch_target(b):
+        first = first_row(b) + b - ZERO_ROWS
+        rows = out_rows[first : first + whole_tiles(b) * P, :]
+        return rows.rearrange("(p t) d -> p t d", t=whole_tiles(b))
+
+    left_source = pos_rows[SEQ - LEFT_ROWS : SEQ, :]
+    left_target = out_rows[SEQ - ZERO_ROWS - LEFT_ROWS : SEQ - ZERO_ROWS, :]
+    zero_target = out_rows[SEQ - ZERO_ROWS :, :].rearrange("(i r) d -> i r d", r=SEQ + 1)[:, 0, :]
+
+    with ExitStack() as ctx:
+        consts = ctx.enter_context(tc.tile_pool(name="consts", bufs=1))
+        x_pool = ctx.enter_context(tc.tile_pool(name="x", bufs=BATCHES))
+        grouped_pool = ctx.enter_context(tc.tile_pool(name="grouped", bufs=2))
+        mx_pool = ctx.enter_context(tc.tile_pool(name="mx", bufs=2))
+        keys_pool = ctx.enter_context(tc.tile_pool(name="keys", bufs=BATCHES * GROUPS))
+        flipped_pool = ctx.enter_context(tc.psum_pool(name="flipped", bufs=4))
+        product_pool = ctx.enter_context(tc.psum_pool(name="product", bufs=4))
+        ctx.enter_context(tc.manual_schedule())
+
+        w_raw = consts.tile([P, D_IN], BF16)
+        nc.scalar.dma_start(out=w_raw[:], in_=W_r)
+        bias_rows = consts.tile([P, D_OUT], BF16)
+        nc.vector.memset(bias_rows[:], 0.0)
+        nc.scalar.dma_start(out=bias_rows[0:1, :], in_=b_r.unsqueeze(0))
+
+        x_batches = []
+        for b in range(BATCHES):
+            x_batch = x_pool.tile([P, TILES, D_IN], BF16, name="x_batch")
+            x_batches.append(x_batch)
+            for first in range(0, TILES, GROUP):
+                last = min(first + GROUP, whole_tiles(b))
+                nc.sync.dma_start(out=x_batch[:, first:last, :], in_=batch_source(b)[:, first:last, :])
+            if b == 0:
+                nc.vector.memset(x_batch[:, TILES - 1, :], 0.0)
+                nc.sync.dma_start(out=x_batch[0:LEFT_ROWS, TILES - 1, :], in_=left_source)
+
+        identity = consts.tile([P, P], F32)
+        make_identity(nc, identity[:])
+
+        w_flipped = flipped_pool.tile([P, FLIPPED_TILES, HALVES, P], F32, name="flipped")
+        transpose_row_tile(nc, identity[:], w_flipped[:, 0], w_raw[:])
+        w_grouped = consts.tile([P, D_OUT * PACK], BF16, align_bytes=64)
+        nc.scalar.copy(
+            out=w_grouped[:].bitcast(F32).rearrange("p (r u) -> p r u", u=HALVES),
+            in_=w_flipped[:, 0].rearrange("p u r -> p r u"),
+        )
+        w_codes = consts.tile([P, D_OUT], U32, align_bytes=64)
+        w_scales = consts.tile([P, D_OUT], U8, align_bytes=64)
+        nc.vector.quantize_mx(out=w_codes[:].bitcast(FP8X4), scales=w_scales[:], in_=w_grouped[:])
+
+        ones = consts.tile([P, P], BF16)
+        nc.vector.memset(ones[:], 1.0)
+        bias_product = product_pool.tile([P, PRODUCT_TILES, D_OUT], F32, name="product")
+        nc.tensor.matmul(out=bias_product[:, 0, :], lhsT=ones[:], rhs=bias_rows[:], start=True, stop=True)
+        bias = consts.tile([P, D_OUT], F32)
+        nc.vector.tensor_copy(out=bias[:], in_=bias_product[:, 0, :])
+
+        def flip_group(g):
+            x_batch = x_batches[g // GROUPS]
+            first = (g % GROUPS) * GROUP
+            grouped = grouped_pool.tile([P, GROUP * P * PACK], BF16, align_bytes=64, name="grouped")
+            grouped_words = grouped[:].bitcast(F32).rearrange("p (t r u) -> p t r u", r=P, u=HALVES)
+            for t in range(0, GROUP, FLIPPED_TILES):
+                flipped = flipped_pool.tile([P, FLIPPED_TILES, HALVES, P], F32, name="flipped")
+                for i in range(FLIPPED_TILES):
+                    transpose_row_tile(nc, identity[:], flipped[:, i], x_batch[:, first + t + i, :])
+                nc.scalar.copy(
+                    out=grouped_words[:, t : t + FLIPPED_TILES],
+                    in_=flipped[:].rearrange("p i u r -> p i r u"),
+                )
+            return grouped
+
+        def quantise_group(grouped):
+            codes = mx_pool.tile([P, GROUP * P], U32, align_bytes=64, name="codes")
+            scales = mx_pool.tile([P, GROUP * P], U8, align_bytes=64, name="scales")
+            nc.vector.quantize_mx(out=codes[:].bitcast(FP8X4), scales=scales[:], in_=grouped[:])
+            return codes, scales
+
+        def multiply_group(g, codes, scales):
+            keys = keys_pool.tile([P, GROUP, D_OUT], F32, name="keys")
+            for t in range(0, GROUP, PRODUCT_TILES):
+                product = product_pool.tile([P, PRODUCT_TILES, D_OUT], F32, name="product")
+                for i in range(PRODUCT_TILES):
+                    rows = slice((t + i) * P, (t + i + 1) * P)
+                    nc.tensor.matmul_mx(
+                        out=product[:, i, :],
+                        lhsT=codes[:, rows].bitcast(FP8X4),
+                        lhsT_scale=scales[:, rows],
+                        rhs=w_codes[:].bitcast(FP8X4),
+                        rhs_scale=w_scales[:],
+                        start=True,
+                        stop=True,
+                    )
+                nc.vector.tensor_add(
+                    out=keys[:, t : t + PRODUCT_TILES, :],
+                    in0=product[:],
+                    in1=bias[:].unsqueeze(1).to_broadcast([P, PRODUCT_TILES, D_OUT]),
+                )
+            b = g // GROUPS
+            first = (g % GROUPS) * GROUP
+            last = min(first + GROUP, whole_tiles(b))
+            nc.sync.dma_start(out=batch_target(b)[:, first:last, :], in_=keys[:, 0 : last - first, :])
+            if last < first + GROUP:
+                nc.sync.dma_start(out=left_target, in_=keys[0:LEFT_ROWS, GROUP - 1, :])
+                nc.sync.dma_start(out=zero_target, in_=keys[LEFT_ROWS:P, GROUP - 1, :])
+
+        waiting = quantise_group(flip_group(0))
+        for g in range(1, BATCHES * GROUPS):
+            fresh = quantise_group(flip_group(g))
+            multiply_group(g - 1, *waiting)
+            waiting = fresh
+        multiply_group(BATCHES * GROUPS - 1, *waiting)

@@ -66,7 +66,7 @@ def tile_relativemultiheadattention_pa_t_kernel(tc, pos_embed, W_r, b_r, out):
         x_pool = ctx.enter_context(tc.tile_pool(name="x", bufs=BATCHES))
         grouped_pool = ctx.enter_context(tc.tile_pool(name="grouped", bufs=2))
         mx_pool = ctx.enter_context(tc.tile_pool(name="mx", bufs=2))
-        keys_pool = ctx.enter_context(tc.tile_pool(name="keys", bufs=BATCHES * GROUPS))
+        keys_pool = ctx.enter_context(tc.tile_pool(name="keys", bufs=BATCHES))
         flipped_pool = ctx.enter_context(tc.psum_pool(name="flipped", bufs=4))
         product_pool = ctx.enter_context(tc.psum_pool(name="product", bufs=4))
         ctx.enter_context(tc.manual_schedule())
@@ -81,8 +81,9 @@ def tile_relativemultiheadattention_pa_t_kernel(tc, pos_embed, W_r, b_r, out):
         for b in range(BATCHES):
             x_batch = x_pool.tile([P, TILES, D_IN], BF16, name="x_batch")
             x_batches.append(x_batch)
-            for first in range(0, TILES, GROUP):
-                last = min(first + GROUP, whole_tiles(b))
+            step = GROUP if b == 0 else TILES
+            for first in range(0, TILES, step):
+                last = min(first + step, whole_tiles(b))
                 nc.sync.dma_start(out=x_batch[:, first:last, :], in_=batch_source(b)[:, first:last, :])
             if b == 0:
                 nc.vector.memset(x_batch[:, TILES - 1, :], 0.0)
@@ -130,8 +131,14 @@ def tile_relativemultiheadattention_pa_t_kernel(tc, pos_embed, W_r, b_r, out):
             nc.vector.quantize_mx(out=codes[:].bitcast(FP8X4), scales=scales[:], in_=grouped[:])
             return codes, scales
 
+        keys_batches = []
+
         def multiply_group(g, codes, scales):
-            keys = keys_pool.tile([P, GROUP, D_OUT], F32, name="keys")
+            b = g // GROUPS
+            first = (g % GROUPS) * GROUP
+            if first == 0:
+                keys_batches.append(keys_pool.tile([P, TILES, D_OUT], F32, name="keys"))
+            keys = keys_batches[b]
             for t in range(0, GROUP, PRODUCT_TILES):
                 product = product_pool.tile([P, PRODUCT_TILES, D_OUT], F32, name="product")
                 for i in range(PRODUCT_TILES):
@@ -146,21 +153,23 @@ def tile_relativemultiheadattention_pa_t_kernel(tc, pos_embed, W_r, b_r, out):
                         stop=True,
                     )
                 nc.vector.tensor_add(
-                    out=keys[:, t : t + PRODUCT_TILES, :],
+                    out=keys[:, first + t : first + t + PRODUCT_TILES, :],
                     in0=product[:],
                     in1=bias[:].unsqueeze(1).to_broadcast([P, PRODUCT_TILES, D_OUT]),
                 )
-            b = g // GROUPS
-            first = (g % GROUPS) * GROUP
-            last = min(first + GROUP, whole_tiles(b))
-            nc.sync.dma_start(out=batch_target(b)[:, first:last, :], in_=keys[:, 0 : last - first, :])
-            if last < first + GROUP:
-                nc.sync.dma_start(out=left_target, in_=keys[0:LEFT_ROWS, GROUP - 1, :])
-                nc.sync.dma_start(out=zero_target, in_=keys[LEFT_ROWS:P, GROUP - 1, :])
+            if first + GROUP == TILES:
+                nc.sync.dma_start(out=batch_target(b), in_=keys[:, 0 : whole_tiles(b), :])
+                if b == 0:
+                    nc.sync.dma_start(out=left_target, in_=keys[0:LEFT_ROWS, TILES - 1, :])
+                    nc.sync.dma_start(out=zero_target, in_=keys[LEFT_ROWS:P, TILES - 1, :])
 
-        waiting = quantise_group(flip_group(0))
-        for g in range(1, BATCHES * GROUPS):
-            fresh = quantise_group(flip_group(g))
-            multiply_group(g - 1, *waiting)
-            waiting = fresh
-        multiply_group(BATCHES * GROUPS - 1, *waiting)
+        n_groups = BATCHES * GROUPS
+        flipped_groups = {}
+        quantised_groups = {}
+        for g in range(n_groups + 2):
+            if g < n_groups:
+                flipped_groups[g] = flip_group(g)
+            if 1 <= g <= n_groups:
+                quantised_groups[g - 1] = quantise_group(flipped_groups[g - 1])
+            if g >= 2:
+                multiply_group(g - 2, *quantised_groups[g - 2])

@@ -81,7 +81,7 @@ def tile_relativemultiheadattention_pa_t_kernel(tc, pos_embed, W_r, b_r, out):
         for b in range(BATCHES):
             x_batch = x_pool.tile([P, TILES, D_IN], BF16, name="x_batch")
             x_batches.append(x_batch)
-            step = GROUP if b == 0 else TILES
+            step = GROUP // 2 if b == 0 else TILES
             for first in range(0, TILES, step):
                 last = min(first + step, whole_tiles(b))
                 nc.sync.dma_start(out=x_batch[:, first:last, :], in_=batch_source(b)[:, first:last, :])
@@ -157,7 +157,11 @@ def tile_relativemultiheadattention_pa_t_kernel(tc, pos_embed, W_r, b_r, out):
                     in0=product[:],
                     in1=bias[:].unsqueeze(1).to_broadcast([P, PRODUCT_TILES, D_OUT]),
                 )
-            if first + GROUP == TILES:
+            if b == BATCHES - 1:
+                nc.sync.dma_start(
+                    out=batch_target(b)[:, first : first + GROUP, :], in_=keys[:, first : first + GROUP, :]
+                )
+            elif first + GROUP == TILES:
                 nc.sync.dma_start(out=batch_target(b), in_=keys[:, 0 : whole_tiles(b), :])
                 if b == 0:
                     nc.sync.dma_start(out=left_target, in_=keys[0:LEFT_ROWS, TILES - 1, :])

from contextlib import ExitStack

import concourse.mybir as mybir
from concourse.masks import make_identity

BF16 = mybir.dt.bfloat16
F32 = mybir.dt.float32
U32 = mybir.dt.uint32
U8 = mybir.dt.uint8
FP8X4 = mybir.dt.float8_e4m3fn_x4

P = 128
BATCHES = 8
SEQ = 2048
D_IN = 512
D_OUT = 128
PACK = 4
BANK = 512

HALVES = D_IN // 2 // P
TILES = SEQ // P
GROUP = 8
GROUPS = TILES // GROUP
FLIPPED_TILES = BANK // (HALVES * P)
PRODUCT_TILES = BANK // D_OUT

ZERO_ROWS = BATCHES - 1
LEFT_ROWS = SEQ - ZERO_ROWS - (TILES - 1) * P
assert LEFT_ROWS + ZERO_ROWS == P

FLOPS = 2 * BATCHES * SEQ * D_IN * D_OUT


def transpose_row_tile(nc, identity, flipped, row_tile):
    words = row_tile.bitcast(F32)
    for u in range(HALVES):
        nc.tensor.transpose(flipped[:, u, :], words[:, u * P : (u + 1) * P], identity)


def tile_relativemultiheadattention_pa_t_kernel(tc, pos_embed, W_r, b_r, out):
    nc = tc.nc
    pos_rows = pos_embed.flatten_outer_dims()
    out_rows = out.flatten_outer_dims()

    def whole_tiles(b):
        return TILES - 1 if b == 0 else TILES

    def first_row(b):
        return ZERO_ROWS if b == 0 else SEQ * b

    def batch_source(b):
        rows = pos_rows[first_row(b) : first_row(b) + whole_tiles(b) * P, :]
        return rows.rearrange("(p t) k -> p t k", t=whole_tiles(b))

    def batch_target(b):
        first = first_row(b) + b - ZERO_ROWS
        rows = out_rows[first : first + whole_tiles(b) * P, :]
        return rows.rearrange("(p t) d -> p t d", t=whole_tiles(b))

    left_source = pos_rows[SEQ - LEFT_ROWS : SEQ, :]
    left_target = out_rows[SEQ - ZERO_ROWS - LEFT_ROWS : SEQ - ZERO_ROWS, :]
    zero_target = out_rows[SEQ - ZERO_ROWS :, :].rearrange("(i r) d -> i r d", r=SEQ + 1)[:, 0, :]

    with ExitStack() as ctx:
        consts = ctx.enter_context(tc.tile_pool(name="consts", bufs=1))
        x_pool = ctx.enter_context(tc.tile_pool(name="x", bufs=BATCHES))
        grouped_pool = ctx.enter_context(tc.tile_pool(name="grouped", bufs=2))
        mx_pool = ctx.enter_context(tc.tile_pool(name="mx", bufs=2))
        keys_pool = ctx.enter_context(tc.tile_pool(name="keys", bufs=BATCHES))
        flipped_pool = ctx.enter_context(tc.psum_pool(name="flipped", bufs=4))
        product_pool = ctx.enter_context(tc.psum_pool(name="product", bufs=4))
        ctx.enter_context(tc.manual_schedule())

        w_raw = consts.tile([P, D_IN], BF16)
        nc.scalar.dma_start(out=w_raw[:], in_=W_r)
        bias_rows = consts.tile([P, D_OUT], BF16)
        nc.vector.memset(bias_rows[:], 0.0)
        nc.scalar.dma_start(out=bias_rows[0:1, :], in_=b_r.unsqueeze(0))

        x_batches = []
        for b in range(BATCHES):
            x_batch = x_pool.tile([P, TILES, D_IN], BF16, name="x_batch")
            x_batches.append(x_batch)
            step = GROUP // 2 if b == 0 else TILES
            for first in range(0, TILES, step):
                last = min(first + step, whole_tiles(b))
                nc.sync.dma_start(out=x_batch[:, first:last, :], in_=batch_source(b)[:, first:last, :])
            if b == 0:
                nc.vector.memset(x_batch[:, TILES - 1, :], 0.0)
                nc.sync.dma_start(out=x_batch[0:LEFT_ROWS, TILES - 1, :], in_=left_source)

        identity = consts.tile([P, P], F32)
        make_identity(nc, identity[:])

        w_flipped = flipped_pool.tile([P, FLIPPED_TILES, HALVES, P], F32, name="flipped")
        transpose_row_tile(nc, identity[:], w_flipped[:, 0], w_raw[:])
        w_grouped = consts.tile([P, D_OUT * PACK], BF16, align_bytes=64)
        nc.scalar.copy(
            out=w_grouped[:].bitcast(F32).rearrange("p (r u) -> p r u", u=HALVES),
            in_=w_flipped[:, 0].rearrange("p u r -> p r u"),
        )
        w_codes = consts.tile([P, D_OUT], U32, align_bytes=64)
        w_scales = consts.tile([P, D_OUT], U8, align_bytes=64)
        nc.vector.quantize_mx(out=w_codes[:].bitcast(FP8X4), scales=w_scales[:], in_=w_grouped[:])

        ones = consts.tile([P, P], BF16)
        nc.vector.memset(ones[:], 1.0)
        bias_product = product_pool.tile([P, PRODUCT_TILES, D_OUT], F32, name="product")
        nc.tensor.matmul(out=bias_product[:, 0, :], lhsT=ones[:], rhs=bias_rows[:], start=True, stop=True)
        bias = consts.tile([P, D_OUT], F32)
        nc.vector.tensor_copy(out=bias[:], in_=bias_product[:, 0, :])

        def flip_group(g):
            x_batch = x_batches[g // GROUPS]
            first = (g % GROUPS) * GROUP
            grouped = grouped_pool.tile([P, GROUP * P * PACK], BF16, align_bytes=64, name="grouped")
            grouped_words = grouped[:].bitcast(F32).rearrange("p (t r u) -> p t r u", r=P, u=HALVES)
            for t in range(0, GROUP, FLIPPED_TILES):
                flipped = flipped_pool.tile([P, FLIPPED_TILES, HALVES, P], F32, name="flipped")
                for i in range(FLIPPED_TILES):
                    transpose_row_tile(nc, identity[:], flipped[:, i], x_batch[:, first + t + i, :])
                nc.scalar.copy(
                    out=grouped_words[:, t : t + FLIPPED_TILES],
                    in_=flipped[:].rearrange("p i u r -> p i r u"),
                )
            return grouped

        def quantise_group(grouped):
            codes = mx_pool.tile([P, GROUP * P], U32, align_bytes=64, name="codes")
            scales = mx_pool.tile([P, GROUP * P], U8, align_bytes=64, name="scales")
            nc.vector.quantize_mx(out=codes[:].bitcast(FP8X4), scales=scales[:], in_=grouped[:])
            return codes, scales

        keys_batches = []

        def multiply_group(g, codes, scales):
            b = g // GROUPS
            first = (g % GROUPS) * GROUP
            if first == 0:
                keys_batches.append(keys_pool.tile([P, TILES, D_OUT], F32, name="keys"))
            keys = keys_batches[b]
            for t in range(0, GROUP, PRODUCT_TILES):
                product = product_pool.tile([P, PRODUCT_TILES, D_OUT], F32, name="product")
                for i in range(PRODUCT_TILES):
                    rows = slice((t + i) * P, (t + i + 1) * P)
                    nc.tensor.matmul_mx(
                        out=product[:, i, :],
                        lhsT=codes[:, rows].bitcast(FP8X4),
                        lhsT_scale=scales[:, rows],
                        rhs=w_codes[:].bitcast(FP8X4),
                        rhs_scale=w_scales[:],
                        start=True,
                        stop=True,
                    )
                nc.vector.tensor_add(
                    out=keys[:, first + t : first + t + PRODUCT_TILES, :],
                    in0=product[:],
                    in1=bias[:].unsqueeze(1).to_broadcast([P, PRODUCT_TILES, D_OUT]),
                )
            if b == BATCHES - 1:
                nc.sync.dma_start(
                    out=batch_target(b)[:, first : first + GROUP, :], in_=keys[:, first : first + GROUP, :]
                )
            elif first + GROUP == TILES:
                nc.sync.dma_start(out=batch_target(b), in_=keys[:, 0 : whole_tiles(b), :])
                if b == 0:
                    nc.sync.dma_start(out=left_target, in_=keys[0:LEFT_ROWS, TILES - 1, :])
                    nc.sync.dma_start(out=zero_target, in_=keys[LEFT_ROWS:P, TILES - 1, :])

        n_groups = BATCHES * GROUPS
        flipped_groups = {}
        quantised_groups = {}
        for g in range(n_groups + 2):
            if g < n_groups:
                flipped_groups[g] = flip_group(g)
            if 1 <= g <= n_groups:
                quantised_groups[g - 1] = quantise_group(flipped_groups[g - 1])
            if g >= 2:
                multiply_group(g - 2, *quantised_groups[g - 2])
